import numpy as np
import ml_dtypes


def mxq(x, axis, fmt="e4m3"):
    dtype, down = {"e4m3": (ml_dtypes.float8_e4m3fn, 7), "e5m2": (ml_dtypes.float8_e5m2, 14)}[fmt]
    v = np.moveaxis(np.asarray(x, np.float32).astype(ml_dtypes.bfloat16).astype(np.float64), axis, -1)
    blocks = v.reshape(v.shape[:-1] + (-1, 32))
    amax = np.abs(blocks).max(-1, keepdims=True)
    byte = np.maximum(np.where(amax > 0, np.frexp(amax)[1] - 1 + 127, 0) - down, 1)
    scale = np.exp2(byte - 127.0)
    codes = (blocks / scale).astype(np.float32).astype(dtype).astype(np.float64)
    return np.moveaxis((codes * scale).reshape(v.shape), -1, axis)


WIDE = False


def mx_kscale(k):
    if not WIDE:
        return np.ones(k)
    levels = np.array([20, -20, 10, -10, 0])
    a = np.random.permutation(np.resize(levels, k // 512 * 4)).reshape(k // 512, 4)
    idx = np.arange(k)
    return np.exp2(a[idx // 512, idx % 128 // 32])


BF16 = ml_dtypes.bfloat16


def bf(x):
    return np.asarray(x, np.float32).astype(BF16)


def f64(x):
    return np.asarray(x).astype(np.float64)


G, GI, GO, B = 32, 32, 16, 8192
K = G * GI
N = G * GO


def build_mask():
    mask = np.ones((N, K))
    for g in range(G):
        mask[g * GO:(g + 1) * GO, g * GI:(g + 1) * GI] = 0.0
    return mask


def setup_inputs():
    s = mx_kscale(B)[:, None]
    bound = 1.0 / np.sqrt(K)
    W = np.random.uniform(-bound, bound, (N, K)) * build_mask()
    data = np.random.standard_normal((B, K)) * s
    b = np.random.standard_normal(N) * 0.3
    g = np.random.standard_normal((B, N)) * np.exp2(np.random.randint(-12, 1, (B, 1))) * 0.25 / s
    return {"data": bf(data), "W": bf(W), "b": bf(b), "grad_out": bf(g)}


def reference(data, W, b, grad_out):
    return mxq(f64(grad_out), 0, "e5m2").T @ mxq(f64(data), 0, "e4m3")

@@ -1,0 +1,117 @@
+from contextlib import ExitStack
+
+import concourse.mybir as mybir
+
+BF16 = mybir.dt.bfloat16
+F32 = mybir.dt.float32
+U32 = mybir.dt.uint32
+U8 = mybir.dt.uint8
+E4M3X4 = mybir.dt.float8_e4m3fn_x4
+E5M2X4 = mybir.dt.float8_e5m2_x4
+
+P = 128
+PACK = 4
+K_PASS = P * PACK
+TOKENS = 8192
+N_IN = 1024
+N_OUT = 512
+PASSES = TOKENS // K_PASS
+N_TILE = 512
+M_TILES = N_OUT // P
+N_TILES = N_IN // N_TILE
+
+FLOPS = 2 * TOKENS * N_IN * N_OUT
+BYTES = 2 * TOKENS * (N_IN + N_OUT) + 4 * N_IN * N_OUT
+
+PINNED = True
+RAW_BUFS = 6
+SCALAR_COLS = 256
+
+
+def regroup(copy, dst, src):
+    copy(
+        out=dst.rearrange("p (c i) t -> p c t i", i=4),
+        in_=src.rearrange("p t (c i) -> p c t i", i=4),
+    )
+
+
+def tile_groupfc_t_kernel(tc, data, W, b, grad_out, out):
+    nc = tc.nc
+    with ExitStack() as ctx:
+        if PINNED:
+            ctx.enter_context(tc.manual_schedule())
+        raw = ctx.enter_context(tc.tile_pool(name="raw", bufs=RAW_BUFS))
+        grouped = ctx.enter_context(tc.tile_pool(name="grouped", bufs=3))
+        codes = ctx.enter_context(tc.tile_pool(name="codes", bufs=3))
+        results = ctx.enter_context(tc.tile_pool(name="results", bufs=1))
+        psum = ctx.enter_context(tc.psum_pool(name="psum", bufs=1))
+
+        acc = [
+            [psum.tile([P, N_TILE], F32, name="acc_%d_%d" % (m, n)) for n in range(N_TILES)]
+            for m in range(M_TILES)
+        ]
+        raw_tiles = {}
+
+        def load(c):
+            g_raw = raw.tile([P, PACK, N_OUT], BF16, tag="g_raw")
+            nc.sync.dma_start(
+                out=g_raw[:],
+                in_=grad_out[c * K_PASS : (c + 1) * K_PASS, :].rearrange("(p j) w -> p j w", j=PACK),
+            )
+            d_raw = raw.tile([P, PACK, N_IN], BF16, tag="d_raw")
+            nc.sync.dma_start(
+                out=d_raw[:],
+                in_=data[c * K_PASS : (c + 1) * K_PASS, :].rearrange("(p j) w -> p j w", j=PACK),
+            )
+            raw_tiles[c] = (g_raw, d_raw)
+
+        for c in range(min(RAW_BUFS, PASSES)):
+            load(c)
+
+        for c in range(PASSES):
+            g_raw, d_raw = raw_tiles[c]
+            g_grp = grouped.tile([P, N_OUT, PACK], BF16, tag="g_grp", align_bytes=64)
+            d_grp = grouped.tile([P, N_IN, PACK], BF16, tag="d_grp", align_bytes=64)
+            regroup(nc.scalar.copy, g_grp[:], g_raw[:])
+            regroup(nc.scalar.copy, d_grp[:, :SCALAR_COLS, :], d_raw[:, :, :SCALAR_COLS])
+            regroup(nc.vector.tensor_copy, d_grp[:, SCALAR_COLS:, :], d_raw[:, :, SCALAR_COLS:])
+
+            g_codes = codes.tile([P, N_OUT], U32, tag="g_codes", align_bytes=64)
+            g_scales = codes.tile([P, N_OUT], U8, tag="g_scales", align_bytes=64)
+            d_codes = codes.tile([P, N_IN], U32, tag="d_codes", align_bytes=64)
+            d_scales = codes.tile([P, N_IN], U8, tag="d_scales", align_bytes=64)
+            nc.vector.quantize_mx(
+                out=g_codes[:].bitcast(E5M2X4),
+                scales=g_scales[:],
+                in_=g_grp[:].rearrange("p w t -> p (w t)"),
+            )
+            nc.vector.quantize_mx(
+                out=d_codes[:].bitcast(E4M3X4),
+                scales=d_scales[:],
+                in_=d_grp[:].rearrange("p w t -> p (w t)"),
+            )
+            if c + RAW_BUFS < PASSES:
+                load(c + RAW_BUFS)
+
+            for m in range(M_TILES):
+                for n in range(N_TILES):
+                    nc.tensor.matmul_mx(
+                        out=acc[m][n][:],
+                        lhsT=g_codes[:, m * P : (m + 1) * P].bitcast(E5M2X4),
+                        lhsT_scale=g_scales[:, m * P : (m + 1) * P],
+                        rhs=d_codes[:, n * N_TILE : (n + 1) * N_TILE].bitcast(E4M3X4),
+                        rhs_scale=d_scales[:, n * N_TILE : (n + 1) * N_TILE],
+                        start=(c == 0),
+                        stop=(c == PASSES - 1),
+                    )
+
+        for m in range(M_TILES):
+            for n in range(N_TILES):
+                res = results.tile([P, N_TILE], F32, name="res_%d_%d" % (m, n))
+                if n == 0:
+                    nc.vector.tensor_copy(out=res[:], in_=acc[m][n][:])
+                else:
+                    nc.scalar.copy(out=res[:], in_=acc[m][n][:])
+                nc.sync.dma_start(
+                    out=out[m * P : (m + 1) * P, n * N_TILE : (n + 1) * N_TILE], in_=res[:]
+                )

@@ -16,16 +16,20 @@ TOKENS = 8192
 N_IN = 1024
 N_OUT = 512
 PASSES = TOKENS // K_PASS
-N_TILE = 512
+HALF = 512
 M_TILES = N_OUT // P
-N_TILES = N_IN // N_TILE
+N_TILES = N_IN // HALF
 
 FLOPS = 2 * TOKENS * N_IN * N_OUT
 BYTES = 2 * TOKENS * (N_IN + N_OUT) + 4 * N_IN * N_OUT
 
 PINNED = True
-RAW_BUFS = 6
-SCALAR_COLS = 256
+D_BUFS = 6
+H_BUFS = 8
+SCALAR_COLS = 280
+TAIL_PASSES = 2
+TAIL_VECTOR_COLS = 248
+LAST_VECTOR_COLS = 400
 
 
 def regroup(copy, dst, src):
@@ -37,81 +41,147 @@ def regroup(copy, dst, src):
 
 def tile_groupfc_t_kernel(tc, data, W, b, grad_out, out):
     nc = tc.nc
+    steady = PASSES - TAIL_PASSES
     with ExitStack() as ctx:
         if PINNED:
             ctx.enter_context(tc.manual_schedule())
-        raw = ctx.enter_context(tc.tile_pool(name="raw", bufs=RAW_BUFS))
-        grouped = ctx.enter_context(tc.tile_pool(name="grouped", bufs=3))
-        codes = ctx.enter_context(tc.tile_pool(name="codes", bufs=3))
+        raw = ctx.enter_context(tc.tile_pool(name="raw", bufs=1))
+        grouped = ctx.enter_context(tc.tile_pool(name="grouped", bufs=1))
+        codes = ctx.enter_context(tc.tile_pool(name="codes", bufs=1))
         results = ctx.enter_context(tc.tile_pool(name="results", bufs=1))
         psum = ctx.enter_context(tc.psum_pool(name="psum", bufs=1))
 
         acc = [
-            [psum.tile([P, N_TILE], F32, name="acc_%d_%d" % (m, n)) for n in range(N_TILES)]
+            [psum.tile([P, HALF], F32, name="acc_%d_%d" % (m, n)) for n in range(N_TILES)]
             for m in range(M_TILES)
         ]
+
+        tail = list(range(steady, PASSES))
+        load_list = []
+        for c in range(steady):
+            load_list.append(("d", c, 0))
+            load_list.append(("g", c, 0))
+        for c in tail:
+            load_list.append(("g", c, 0))
+        for h in range(N_TILES):
+            for c in tail:
+                load_list.append(("h", c, h))
         raw_tiles = {}
+        state = {"next": 0, "d_alloc": 0, "d_used": 0, "h_alloc": 0, "h_used": 0}
 
-        def load(c):
-            g_raw = raw.tile([P, PACK, N_OUT], BF16, tag="g_raw")
-            nc.sync.dma_start(
-                out=g_raw[:],
-                in_=grad_out[c * K_PASS : (c + 1) * K_PASS, :].rearrange("(p j) w -> p j w", j=PACK),
-            )
-            d_raw = raw.tile([P, PACK, N_IN], BF16, tag="d_raw")
-            nc.sync.dma_start(
-                out=d_raw[:],
-                in_=data[c * K_PASS : (c + 1) * K_PASS, :].rearrange("(p j) w -> p j w", j=PACK),
-            )
-            raw_tiles[c] = (g_raw, d_raw)
+        def pump():
+            while state["next"] < len(load_list):
+                kind, c, h = load_list[state["next"]]
+                rows = slice(c * K_PASS, (c + 1) * K_PASS)
+                if kind == "d":
+                    if state["d_alloc"] - state["d_used"] >= D_BUFS:
+                        return
+                    state["d_alloc"] += 1
+                    t = raw.tile([P, PACK, N_IN], BF16, name="d_raw", tag="d_raw", bufs=D_BUFS)
+                    src = data[rows, :]
+                else:
+                    if state["h_alloc"] - state["h_used"] >= H_BUFS:
+                        return
+                    state["h_alloc"] += 1
+                    t = raw.tile([P, PACK, HALF], BF16, name="h_raw", tag="h_raw", bufs=H_BUFS)
+                    if kind == "g":
+                        src = grad_out[rows, :]
+                    else:
+                        src = data[rows, h * HALF : (h + 1) * HALF]
+                nc.sync.dma_start(out=t[:], in_=src.rearrange("(p j) w -> p j w", j=PACK))
+                raw_tiles[(kind, c, h)] = t
+                state["next"] += 1
 
-        for c in range(min(RAW_BUFS, PASSES)):
-            load(c)
+        def half_codes():
+            words = codes.tile([P, HALF], U32, name="h_codes", tag="h_codes", bufs=8, align_bytes=64)
+            plane = codes.tile([P, HALF], U8, name="h_scales", tag="h_scales", bufs=8, align_bytes=64)
+            return words, plane
 
-        for c in range(PASSES):
-            g_raw, d_raw = raw_tiles[c]
-            g_grp = grouped.tile([P, N_OUT, PACK], BF16, tag="g_grp", align_bytes=64)
-            d_grp = grouped.tile([P, N_IN, PACK], BF16, tag="d_grp", align_bytes=64)
-            regroup(nc.scalar.copy, g_grp[:], g_raw[:])
-            regroup(nc.scalar.copy, d_grp[:, :SCALAR_COLS, :], d_raw[:, :, :SCALAR_COLS])
-            regroup(nc.vector.tensor_copy, d_grp[:, SCALAR_COLS:, :], d_raw[:, :, SCALAR_COLS:])
-
-            g_codes = codes.tile([P, N_OUT], U32, tag="g_codes", align_bytes=64)
-            g_scales = codes.tile([P, N_OUT], U8, tag="g_scales", align_bytes=64)
-            d_codes = codes.tile([P, N_IN], U32, tag="d_codes", align_bytes=64)
-            d_scales = codes.tile([P, N_IN], U8, tag="d_scales", align_bytes=64)
+        def quantise(grp, words, plane, fmt):
             nc.vector.quantize_mx(
-                out=g_codes[:].bitcast(E5M2X4),
-                scales=g_scales[:],
-                in_=g_grp[:].rearrange("p w t -> p (w t)"),
+                out=words[:].bitcast(fmt), scales=plane[:], in_=grp[:].rearrange("p w t -> p (w t)")
             )
-            nc.vector.quantize_mx(
-                out=d_codes[:].bitcast(E4M3X4),
-                scales=d_scales[:],
-                in_=d_grp[:].rearrange("p w t -> p (w t)"),
-            )
-            if c + RAW_BUFS < PASSES:
-                load(c + RAW_BUFS)
 
+        def multiply(c, g_q, d_words, d_plane, n):
+            g_words, g_plane = g_q
             for m in range(M_TILES):
-                for n in range(N_TILES):
-                    nc.tensor.matmul_mx(
-                        out=acc[m][n][:],
-                        lhsT=g_codes[:, m * P : (m + 1) * P].bitcast(E5M2X4),
-                        lhsT_scale=g_scales[:, m * P : (m + 1) * P],
-                        rhs=d_codes[:, n * N_TILE : (n + 1) * N_TILE].bitcast(E4M3X4),
-                        rhs_scale=d_scales[:, n * N_TILE : (n + 1) * N_TILE],
-                        start=(c == 0),
-                        stop=(c == PASSES - 1),
-                    )
+                nc.tensor.matmul_mx(
+                    out=acc[m][n][:],
+                    lhsT=g_words[:, m * P : (m + 1) * P].bitcast(E5M2X4),
+                    lhsT_scale=g_plane[:, m * P : (m + 1) * P],
+                    rhs=d_words.bitcast(E4M3X4),
+                    rhs_scale=d_plane,
+                    start=(c == 0),
+                    stop=(c == PASSES - 1),
+                )
 
-        for m in range(M_TILES):
+        pump()
+        g_grp = {}
+        g_q = {}
+        d_q = {}
+
+        def finish_steady(c):
+            g_q[c] = half_codes()
+            quantise(g_grp[c], g_q[c][0], g_q[c][1], E5M2X4)
+
+        def multiply_steady(c):
             for n in range(N_TILES):
-                res = results.tile([P, N_TILE], F32, name="res_%d_%d" % (m, n))
-                if n == 0:
+                cols = slice(n * HALF, (n + 1) * HALF)
+                multiply(c, g_q[c], d_q[c][0][:, cols], d_q[c][1][:, cols], n)
+
+        for c in range(steady):
+            d_raw = raw_tiles[("d", c, 0)]
+            g_raw = raw_tiles[("g", c, 0)]
+            d_grp = grouped.tile([P, N_IN, PACK], BF16, name="d_grp", tag="d_grp", bufs=3, align_bytes=64)
+            g_grp[c] = grouped.tile([P, HALF, PACK], BF16, name="h_grp", tag="h_grp", bufs=4, align_bytes=64)
+            regroup(nc.scalar.copy, d_grp[:, :SCALAR_COLS, :], d_raw[:, :, :SCALAR_COLS])
+            regroup(nc.scalar.copy, g_grp[c][:], g_raw[:])
+            regroup(nc.vector.tensor_copy, d_grp[:, SCALAR_COLS:, :], d_raw[:, :, SCALAR_COLS:])
+            state["d_used"] += 1
+            state["h_used"] += 1
+            if c > 0:
+                finish_steady(c - 1)
+            d_words = codes.tile([P, N_IN], U32, name="d_codes", tag="d_codes", bufs=3, align_bytes=64)
+            d_plane = codes.tile([P, N_IN], U8, name="d_scales", tag="d_scales", bufs=3, align_bytes=64)
+            quantise(d_grp, d_words, d_plane, E4M3X4)
+            d_q[c] = (d_words, d_plane)
+            pump()
+            if c > 0:
+                multiply_steady(c - 1)
+
+        pieces = [("g", c, 0) for c in tail] + [("h", c, h) for h in range(N_TILES) for c in tail]
+        piece_grp = {}
+
+        def finish_piece(key):
+            kind, c, h = key
+            q = half_codes()
+            quantise(piece_grp[key], q[0], q[1], E5M2X4 if kind == "g" else E4M3X4)
+            if kind == "g":
+                g_q[c] = q
+            else:
+                multiply(c, g_q[c], q[0][:], q[1][:], h)
+
+        for i, key in enumerate(pieces):
+            v_cols = LAST_VECTOR_COLS if i == len(pieces) - 1 else TAIL_VECTOR_COLS
+            src = raw_tiles[key]
+            grp = grouped.tile([P, HALF, PACK], BF16, name="h_grp", tag="h_grp", bufs=4, align_bytes=64)
+            piece_grp[key] = grp
+            regroup(nc.scalar.copy, grp[:, v_cols:, :], src[:, :, v_cols:])
+            regroup(nc.vector.tensor_copy, grp[:, :v_cols, :], src[:, :, :v_cols])
+            state["h_used"] += 1
+            pump()
+            if i == 0:
+                finish_steady(steady - 1)
+                multiply_steady(steady - 1)
+            else:
+                finish_piece(pieces[i - 1])
+        finish_piece(pieces[-1])
+
+        for n in range(N_TILES):
+            for m in range(M_TILES):
+                res = results.tile([P, HALF], F32, name="res_%d_%d" % (m, n))
+                if n == 1 and m % 2 == 0:
                     nc.vector.tensor_copy(out=res[:], in_=acc[m][n][:])
                 else:
                     nc.scalar.copy(out=res[:], in_=acc[m][n][:])
-                nc.sync.dma_start(
-                    out=out[m * P : (m + 1) * P, n * N_TILE : (n + 1) * N_TILE], in_=res[:]
-                )
+                nc.sync.dma_start(out=out[m * P : (m + 1) * P, n * HALF : (n + 1) * HALF], in_=res[:])

@@ -152,14 +152,30 @@ def tile_groupfc_t_kernel(tc, data, W, b, grad_out, out):
         pieces = [("g", c, 0) for c in tail] + [("h", c, h) for h in range(N_TILES) for c in tail]
         piece_grp = {}
 
+        right = []
+
         def finish_piece(key):
             kind, c, h = key
             q = half_codes()
             quantise(piece_grp[key], q[0], q[1], E5M2X4 if kind == "g" else E4M3X4)
             if kind == "g":
                 g_q[c] = q
-            else:
+            elif h == 0:
                 multiply(c, g_q[c], q[0][:], q[1][:], h)
+            else:
+                right.append((c, q))
+                if c == PASSES - 1:
+                    for m in range(M_TILES):
+                        for cc, qq in right:
+                            nc.tensor.matmul_mx(
+                                out=acc[m][h][:],
+                                lhsT=g_q[cc][0][:, m * P : (m + 1) * P].bitcast(E5M2X4),
+                                lhsT_scale=g_q[cc][1][:, m * P : (m + 1) * P],
+                                rhs=qq[0][:].bitcast(E4M3X4),
+                                rhs_scale=qq[1][:],
+                                start=False,
+                                stop=(cc == PASSES - 1),
+                            )
 
         for i, key in enumerate(pieces):
             v_cols = LAST_VECTOR_COLS if i == len(pieces) - 1 else TAIL_VECTOR_COLS

@@ -26,16 +26,16 @@ BYTES = 2 * TOKENS * (N_IN + N_OUT) + 4 * N_IN * N_OUT
 PINNED = True
 D_BUFS = 6
 H_BUFS = 8
-SCALAR_COLS = 280
+SCALAR_COLS = 272
 TAIL_PASSES = 2
-TAIL_VECTOR_COLS = 248
+TAIL_VECTOR_COLS = 256
 LAST_VECTOR_COLS = 400
 
 
 def regroup(copy, dst, src):
     copy(
-        out=dst.rearrange("p (c i) t -> p c t i", i=4),
-        in_=src.rearrange("p t (c i) -> p c t i", i=4),
+        out=dst.rearrange("p (c i) t -> p c t i", i=8),
+        in_=src.rearrange("p t (c i) -> p c t i", i=8),
     )
 
 

from contextlib import ExitStack

import concourse.mybir as mybir

BF16 = mybir.dt.bfloat16
F32 = mybir.dt.float32
U32 = mybir.dt.uint32
U8 = mybir.dt.uint8
E4M3X4 = mybir.dt.float8_e4m3fn_x4
E5M2X4 = mybir.dt.float8_e5m2_x4

P = 128
PACK = 4
K_PASS = P * PACK
TOKENS = 8192
N_IN = 1024
N_OUT = 512
PASSES = TOKENS // K_PASS
HALF = 512
M_TILES = N_OUT // P
N_TILES = N_IN // HALF

FLOPS = 2 * TOKENS * N_IN * N_OUT
BYTES = 2 * TOKENS * (N_IN + N_OUT) + 4 * N_IN * N_OUT

PINNED = True
D_BUFS = 6
H_BUFS = 8
SCALAR_COLS = 272
TAIL_PASSES = 2
TAIL_VECTOR_COLS = 256
LAST_VECTOR_COLS = 400


def regroup(copy, dst, src):
    copy(
        out=dst.rearrange("p (c i) t -> p c t i", i=8),
        in_=src.rearrange("p t (c i) -> p c t i", i=8),
    )


def tile_groupfc_t_kernel(tc, data, W, b, grad_out, out):
    nc = tc.nc
    steady = PASSES - TAIL_PASSES
    with ExitStack() as ctx:
        if PINNED:
            ctx.enter_context(tc.manual_schedule())
        raw = ctx.enter_context(tc.tile_pool(name="raw", bufs=1))
        grouped = ctx.enter_context(tc.tile_pool(name="grouped", bufs=1))
        codes = ctx.enter_context(tc.tile_pool(name="codes", bufs=1))
        results = ctx.enter_context(tc.tile_pool(name="results", bufs=1))
        psum = ctx.enter_context(tc.psum_pool(name="psum", bufs=1))

        acc = [
            [psum.tile([P, HALF], F32, name="acc_%d_%d" % (m, n)) for n in range(N_TILES)]
            for m in range(M_TILES)
        ]

        tail = list(range(steady, PASSES))
        load_list = []
        for c in range(steady):
            load_list.append(("d", c, 0))
            load_list.append(("g", c, 0))
        for c in tail:
            load_list.append(("g", c, 0))
        for h in range(N_TILES):
            for c in tail:
                load_list.append(("h", c, h))
        raw_tiles = {}
        state = {"next": 0, "d_alloc": 0, "d_used": 0, "h_alloc": 0, "h_used": 0}

        def pump():
            while state["next"] < len(load_list):
                kind, c, h = load_list[state["next"]]
                rows = slice(c * K_PASS, (c + 1) * K_PASS)
                if kind == "d":
                    if state["d_alloc"] - state["d_used"] >= D_BUFS:
                        return
                    state["d_alloc"] += 1
                    t = raw.tile([P, PACK, N_IN], BF16, name="d_raw", tag="d_raw", bufs=D_BUFS)
                    src = data[rows, :]
                else:
                    if state["h_alloc"] - state["h_used"] >= H_BUFS:
                        return
                    state["h_alloc"] += 1
                    t = raw.tile([P, PACK, HALF], BF16, name="h_raw", tag="h_raw", bufs=H_BUFS)
                    if kind == "g":
                        src = grad_out[rows, :]
                    else:
                        src = data[rows, h * HALF : (h + 1) * HALF]
                nc.sync.dma_start(out=t[:], in_=src.rearrange("(p j) w -> p j w", j=PACK))
                raw_tiles[(kind, c, h)] = t
                state["next"] += 1

        def half_codes():
            words = codes.tile([P, HALF], U32, name="h_codes", tag="h_codes", bufs=8, align_bytes=64)
            plane = codes.tile([P, HALF], U8, name="h_scales", tag="h_scales", bufs=8, align_bytes=64)
            return words, plane

        def quantise(grp, words, plane, fmt):
            nc.vector.quantize_mx(
                out=words[:].bitcast(fmt), scales=plane[:], in_=grp[:].rearrange("p w t -> p (w t)")
            )

        def multiply(c, g_q, d_words, d_plane, n):
            g_words, g_plane = g_q
            for m in range(M_TILES):
                nc.tensor.matmul_mx(
                    out=acc[m][n][:],
                    lhsT=g_words[:, m * P : (m + 1) * P].bitcast(E5M2X4),
                    lhsT_scale=g_plane[:, m * P : (m + 1) * P],
                    rhs=d_words.bitcast(E4M3X4),
                    rhs_scale=d_plane,
                    start=(c == 0),
                    stop=(c == PASSES - 1),
                )

        pump()
        g_grp = {}
        g_q = {}
        d_q = {}

        def finish_steady(c):
            g_q[c] = half_codes()
            quantise(g_grp[c], g_q[c][0], g_q[c][1], E5M2X4)

        def multiply_steady(c):
            for n in range(N_TILES):
                cols = slice(n * HALF, (n + 1) * HALF)
                multiply(c, g_q[c], d_q[c][0][:, cols], d_q[c][1][:, cols], n)

        for c in range(steady):
            d_raw = raw_tiles[("d", c, 0)]
            g_raw = raw_tiles[("g", c, 0)]
            d_grp = grouped.tile([P, N_IN, PACK], BF16, name="d_grp", tag="d_grp", bufs=3, align_bytes=64)
            g_grp[c] = grouped.tile([P, HALF, PACK], BF16, name="h_grp", tag="h_grp", bufs=4, align_bytes=64)
            regroup(nc.scalar.copy, d_grp[:, :SCALAR_COLS, :], d_raw[:, :, :SCALAR_COLS])
            regroup(nc.scalar.copy, g_grp[c][:], g_raw[:])
            regroup(nc.vector.tensor_copy, d_grp[:, SCALAR_COLS:, :], d_raw[:, :, SCALAR_COLS:])
            state["d_used"] += 1
            state["h_used"] += 1
            if c > 0:
                finish_steady(c - 1)
            d_words = codes.tile([P, N_IN], U32, name="d_codes", tag="d_codes", bufs=3, align_bytes=64)
            d_plane = codes.tile([P, N_IN], U8, name="d_scales", tag="d_scales", bufs=3, align_bytes=64)
            quantise(d_grp, d_words, d_plane, E4M3X4)
            d_q[c] = (d_words, d_plane)
            pump()
            if c > 0:
                multiply_steady(c - 1)

        pieces = [("g", c, 0) for c in tail] + [("h", c, h) for h in range(N_TILES) for c in tail]
        piece_grp = {}

        right = []

        def finish_piece(key):
            kind, c, h = key
            q = half_codes()
            quantise(piece_grp[key], q[0], q[1], E5M2X4 if kind == "g" else E4M3X4)
            if kind == "g":
                g_q[c] = q
            elif h == 0:
                multiply(c, g_q[c], q[0][:], q[1][:], h)
            else:
                right.append((c, q))
                if c == PASSES - 1:
                    for m in range(M_TILES):
                        for cc, qq in right:
                            nc.tensor.matmul_mx(
                                out=acc[m][h][:],
                                lhsT=g_q[cc][0][:, m * P : (m + 1) * P].bitcast(E5M2X4),
                                lhsT_scale=g_q[cc][1][:, m * P : (m + 1) * P],
                                rhs=qq[0][:].bitcast(E4M3X4),
                                rhs_scale=qq[1][:],
                                start=False,
                                stop=(cc == PASSES - 1),
                            )

        for i, key in enumerate(pieces):
            v_cols = LAST_VECTOR_COLS if i == len(pieces) - 1 else TAIL_VECTOR_COLS
            src = raw_tiles[key]
            grp = grouped.tile([P, HALF, PACK], BF16, name="h_grp", tag="h_grp", bufs=4, align_bytes=64)
            piece_grp[key] = grp
            regroup(nc.scalar.copy, grp[:, v_cols:, :], src[:, :, v_cols:])
            regroup(nc.vector.tensor_copy, grp[:, :v_cols, :], src[:, :, :v_cols])
            state["h_used"] += 1
            pump()
            if i == 0:
                finish_steady(steady - 1)
                multiply_steady(steady - 1)
            else:
                finish_piece(pieces[i - 1])
        finish_piece(pieces[-1])

        for n in range(N_TILES):
            for m in range(M_TILES):
                res = results.tile([P, HALF], F32, name="res_%d_%d" % (m, n))
                if n == 1 and m % 2 == 0:
                    nc.vector.tensor_copy(out=res[:], in_=acc[m][n][:])
                else:
                    nc.scalar.copy(out=res[:], in_=acc[m][n][:])
                nc.sync.dma_start(out=out[m * P : (m + 1) * P, n * HALF : (n + 1) * HALF], in_=res[:])
